import numpy as np
import ml_dtypes


def mxq(x, axis, fmt="e4m3"):
    dtype, down = {"e4m3": (ml_dtypes.float8_e4m3fn, 7), "e5m2": (ml_dtypes.float8_e5m2, 14)}[fmt]
    v = np.moveaxis(np.asarray(x, np.float32).astype(ml_dtypes.bfloat16).astype(np.float64), axis, -1)
    blocks = v.reshape(v.shape[:-1] + (-1, 32))
    amax = np.abs(blocks).max(-1, keepdims=True)
    byte = np.maximum(np.where(amax > 0, np.frexp(amax)[1] - 1 + 127, 0) - down, 1)
    scale = np.exp2(byte - 127.0)
    codes = (blocks / scale).astype(np.float32).astype(dtype).astype(np.float64)
    return np.moveaxis((codes * scale).reshape(v.shape), -1, axis)


WIDE = False


def mx_kscale(k):
    if not WIDE:
        return np.ones(k)
    levels = np.array([10, -10, 5, -5, 0])
    a = np.random.permutation(np.resize(levels, k // 512 * 4)).reshape(k // 512, 4)
    idx = np.arange(k)
    return np.exp2(a[idx // 512, idx % 128 // 32])


BF16 = ml_dtypes.bfloat16


def bf(x):
    return np.asarray(x, np.float32).astype(BF16)


def f64(x):
    return np.asarray(x).astype(np.float64)


B, C, CQ, H, W, D = 1, 1024, 128, 64, 64, 4
HP, WP = H // D, W // D
N = HP * WP


def conv1x1(xq, w, b):
    y = xq @ mxq(f64(w), 1, "e4m3").T
    return y.transpose(0, 2, 1).reshape(B, -1, H, W) + f64(b)[None, :, None, None]


def maxpool(y):
    return y.reshape(B, -1, HP, D, WP, D).max(axis=(3, 5))


def setup_inputs():
    s = mx_kscale(C)
    return {"x": bf(np.random.standard_normal((B, C, H, W)) * s[None, :, None, None]),
            "wq": bf(np.random.standard_normal((CQ, C)) * 0.4 / np.sqrt(C) / s[None, :]),
            "bq": bf(np.random.standard_normal(CQ) * 0.1),
            "wk": bf(np.random.standard_normal((CQ, C)) * 0.4 / np.sqrt(C) / s[None, :]),
            "bk": bf(np.random.standard_normal(CQ) * 0.1),
            "wv": bf(np.random.standard_normal((C, C)) / np.sqrt(C) / s[None, :]),
            "bv": bf(np.random.standard_normal(C) * 0.1)}


def reference(x, wq, bq, wk, bk, wv, bv):
    xq = mxq(f64(x), 1, "e4m3").reshape(B, C, H * W).transpose(0, 2, 1)
    q = maxpool(conv1x1(xq, wq, bq)).reshape(B, -1, N).transpose(0, 2, 1)
    k = maxpool(conv1x1(xq, wk, bk)).reshape(B, -1, N)
    v = maxpool(conv1x1(xq, wv, bv)).reshape(B, C, N)
    return q, k, v

@@ -1,0 +1,195 @@
+from contextlib import ExitStack
+
+import concourse.mybir as mybir
+from concourse.masks import make_identity
+
+F32 = mybir.dt.float32
+BF16 = mybir.dt.bfloat16
+U32 = mybir.dt.uint32
+U8 = mybir.dt.uint8
+FP8X4 = mybir.dt.float8_e4m3fn_x4
+
+P = 128
+PACK = 4
+K_PASS = P * PACK
+CHANNELS = 1024
+PASSES = CHANNELS // K_PASS
+SIDE = 64
+POOL = 4
+CHUNK = 512
+CHUNKS = SIDE * SIDE // CHUNK
+CHUNK_BANDS = CHUNK // (SIDE * POOL)
+BAND_WINDOWS = SIDE // POOL
+CHUNK_WINDOWS = CHUNK_BANDS * BAND_WINDOWS
+WINDOWS = CHUNKS * CHUNK_WINDOWS
+TILES = 10
+HALVES = 2
+HALF_WINDOWS = WINDOWS // HALVES
+HALF_CHUNKS = CHUNKS // HALVES
+LEAD = 5
+QUANTISE_AT = 6
+
+FLOPS = 2 * TILES * P * CHANNELS * SIDE * SIDE
+
+
+def tile_selfattentionpatch_pa_t_kernel(tc, x, wq, bq, wk, bk, wv, bv, out_0, out_1, out_2):
+    nc = tc.nc
+    with ExitStack() as ctx:
+        const = ctx.enter_context(tc.tile_pool(name="const", bufs=1))
+        loaded = ctx.enter_context(tc.tile_pool(name="loaded", bufs=1))
+        stage = ctx.enter_context(tc.tile_pool(name="stage", bufs=3))
+        psum_small = ctx.enter_context(tc.psum_pool(name="psum_small", bufs=2))
+        psum_acc = ctx.enter_context(tc.psum_pool(name="psum_acc", bufs=6))
+        ctx.enter_context(tc.manual_schedule())
+
+        x_pairs = x[0].rearrange("(s p e) h w -> s p e (h w)", s=PASSES * 2, p=P, e=2)
+        w_blocks = [wq, wk] + [wv[i * P : (i + 1) * P, :] for i in range(TILES - 2)]
+        x_raw = [loaded.tile([P, PASSES * PACK, CHUNK], BF16, name="x_raw%d" % j) for j in range(CHUNKS)]
+        w_raw = [loaded.tile([P, CHANNELS], BF16, name="w_raw%d" % m) for m in range(TILES)]
+
+        def load_x(j):
+            for s in range(PASSES * 2):
+                nc.sync.dma_start(
+                    out=x_raw[j][:, 2 * s : 2 * s + 2, :],
+                    in_=x_pairs[s][:, :, j * CHUNK : (j + 1) * CHUNK],
+                )
+
+        load_x(0)
+        for m in range(TILES):
+            nc.sync.dma_start(out=w_raw[m][:], in_=w_blocks[m])
+        for j in range(1, CHUNKS):
+            load_x(j)
+
+        ident = const.tile([P, P], F32)
+        make_identity(nc, ident[:])
+
+        table_in = const.tile([P, 1], F32)
+        table_out = const.tile([P, 1], F32)
+        nc.vector.memset(table_in[:], 0.0)
+        nc.scalar.activation(out=table_out[:], in_=table_in[:], func=mybir.ActivationFunctionType.Identity)
+
+        bias_rows = const.tile([P, P], BF16)
+        nc.gpsimd.memset(bias_rows[:], 0.0)
+        nc.scalar.dma_start(out=bias_rows[0:1, :], in_=bq.unsqueeze(0))
+        nc.scalar.dma_start(out=bias_rows[1:2, :], in_=bk.unsqueeze(0))
+        nc.scalar.dma_start(out=bias_rows[2:TILES, :], in_=bv.rearrange("(r o) -> r o", o=P))
+        bias_rows_f32 = const.tile([P, P], F32)
+        nc.gpsimd.tensor_copy(out=bias_rows_f32[:], in_=bias_rows[:])
+
+        w_codes = const.tile([P, TILES * PASSES * P], U32, align_bytes=64)
+        w_scales = const.tile([P, TILES * PASSES * P], U8, align_bytes=64)
+        pooled = const.tile([P, TILES, WINDOWS], F32)
+        result = const.tile([P, TILES, WINDOWS], F32)
+        bias = const.tile([P, TILES], F32)
+
+        def prepare_weights(m):
+            words = w_raw[m][:].bitcast(F32)
+            flipped = psum_small.tile([P, PASSES * 2 * P], F32, tag="small")
+            for s in range(PASSES * 2):
+                nc.tensor.transpose(flipped[:, s * P : (s + 1) * P], words[:, s * P : (s + 1) * P], ident[:])
+            w_grouped = stage.tile([P, PASSES * P * 2], F32, align_bytes=64)
+            nc.scalar.copy(
+                out=w_grouped[:].rearrange("p (g o u) -> p g o u", g=PASSES, u=2),
+                in_=flipped[:].rearrange("p (g u o) -> p g o u", g=PASSES, u=2),
+            )
+            cols = slice(m * PASSES * P, (m + 1) * PASSES * P)
+            nc.vector.quantize_mx(
+                out=w_codes[:, cols].bitcast(FP8X4), scales=w_scales[:, cols], in_=w_grouped[:].bitcast(BF16)
+            )
+
+        x_grouped = {}
+        x_codes = {}
+        x_scales = {}
+
+        def regroup_x(j):
+            x_grouped[j] = stage.tile([P, PASSES, CHUNK * PACK], BF16, name="x_grouped", align_bytes=64)
+            for g in range(PASSES):
+                source = x_raw[j][:, g * PACK : (g + 1) * PACK, :].rearrange("p t (c i) -> p c t i", i=4)
+                target = x_grouped[j][:, g, :].rearrange("p (c i t) -> p c t i", i=4, t=PACK)
+                if j == 0:
+                    nc.vector.tensor_copy(out=target, in_=source)
+                else:
+                    nc.scalar.copy(out=target, in_=source)
+
+        def quantise_x(j, g):
+            if g == 0:
+                x_codes[j] = stage.tile([P, PASSES * CHUNK], U32, name="x_codes", align_bytes=64)
+                x_scales[j] = stage.tile([P, PASSES * CHUNK], U8, name="x_scales", align_bytes=64)
+            x_cols = slice(g * CHUNK, (g + 1) * CHUNK)
+            nc.vector.quantize_mx(
+                out=x_codes[j][:, x_cols].bitcast(FP8X4), scales=x_scales[j][:, x_cols], in_=x_grouped[j][:, g, :]
+            )
+
+        def convolve_and_pool(j, m):
+            acc = psum_acc.tile([P, CHUNK], F32)
+            for g in range(PASSES):
+                w_cols = slice((m * PASSES + g) * P, (m * PASSES + g + 1) * P)
+                x_cols = slice(g * CHUNK, (g + 1) * CHUNK)
+                nc.tensor.matmul_mx(
+                    out=acc[:],
+                    lhsT=w_codes[:, w_cols].bitcast(FP8X4),
+                    lhsT_scale=w_scales[:, w_cols],
+                    rhs=x_codes[j][:, x_cols].bitcast(FP8X4),
+                    rhs_scale=x_scales[j][:, x_cols],
+                    start=(g == 0),
+                    stop=(g == PASSES - 1),
+                )
+            nc.vector.tensor_reduce(
+                out=pooled[:, m, j * CHUNK_WINDOWS : (j + 1) * CHUNK_WINDOWS].rearrange(
+                    "p (a b) -> p a b", a=CHUNK_BANDS
+                ),
+                in_=acc[:].rearrange("p (a di b dj) -> p a b di dj", a=CHUNK_BANDS, di=POOL, dj=POOL),
+                axis=mybir.AxisListType.XY,
+                op=mybir.AluOpType.max,
+            )
+
+        def prepare_bias():
+            bias_flipped = psum_small.tile([P, P], F32, tag="small")
+            nc.tensor.transpose(bias_flipped[:], bias_rows_f32[:], ident[:])
+            nc.scalar.copy(out=bias[:], in_=bias_flipped[:, 0:TILES])
+
+        def add_bias(m, cols):
+            nc.scalar.activation(
+                out=result[:, m, cols],
+                in_=pooled[:, m, cols],
+                func=mybir.ActivationFunctionType.Identity,
+                bias=bias[:, m : m + 1],
+                scale=1.0,
+            )
+
+        def finish_half(h):
+            cols = slice(h * HALF_WINDOWS, (h + 1) * HALF_WINDOWS)
+            add_bias(0, cols)
+            q_flipped = psum_small.tile([P, P], F32, tag="small")
+            nc.tensor.transpose(q_flipped[:], result[:, 0, cols], ident[:])
+            add_bias(1, cols)
+            nc.sync.dma_start(out=out_1[0, :, cols], in_=result[:, 1, cols])
+            q_rows = stage.tile([P, P], F32)
+            nc.scalar.copy(out=q_rows[:], in_=q_flipped[:])
+            nc.sync.dma_start(out=out_0[0, cols, :], in_=q_rows[:])
+            for m in range(2, TILES):
+                add_bias(m, cols)
+                nc.sync.dma_start(out=out_2[0, (m - 2) * P : (m - 1) * P, cols], in_=result[:, m, cols])
+
+        regroup_x(0)
+        for g in range(PASSES):
+            quantise_x(0, g)
+        for m in range(LEAD):
+            prepare_weights(m)
+        for j in range(CHUNKS):
+            for m in range(TILES):
+                for g in range(PASSES):
+                    if m == QUANTISE_AT + 2 * g and j + 1 < CHUNKS:
+                        quantise_x(j + 1, g)
+                convolve_and_pool(j, m)
+                if j == 0 and m + LEAD < TILES:
+                    prepare_weights(m + LEAD)
+                if m == LEAD:
+                    if j == 0:
+                        regroup_x(1)
+                    if j + 2 < CHUNKS:
+                        regroup_x(j + 2)
+            if j == 0:
+                prepare_bias()
+            if (j + 1) % HALF_CHUNKS == 0:
+                finish_half(j // HALF_CHUNKS)

@@ -26,7 +26,7 @@ TILES = 10
 HALVES = 2
 HALF_WINDOWS = WINDOWS // HALVES
 HALF_CHUNKS = CHUNKS // HALVES
-LEAD = 5
+FIRST_WEIGHTS = 4
 QUANTISE_AT = 6
 
 FLOPS = 2 * TILES * P * CHANNELS * SIDE * SIDE
@@ -54,8 +54,10 @@ def tile_selfattentionpatch_pa_t_kernel(tc, x, wq, bq, wk, bk, wv, bv, out_0, ou
                     in_=x_pairs[s][:, :, j * CHUNK : (j + 1) * CHUNK],
                 )
 
+        for m in range(FIRST_WEIGHTS):
+            nc.sync.dma_start(out=w_raw[m][:], in_=w_blocks[m])
         load_x(0)
-        for m in range(TILES):
+        for m in range(FIRST_WEIGHTS, TILES):
             nc.sync.dma_start(out=w_raw[m][:], in_=w_blocks[m])
         for j in range(1, CHUNKS):
             load_x(j)
@@ -70,9 +72,9 @@ def tile_selfattentionpatch_pa_t_kernel(tc, x, wq, bq, wk, bk, wv, bv, out_0, ou
 
         bias_rows = const.tile([P, P], BF16)
         nc.gpsimd.memset(bias_rows[:], 0.0)
-        nc.scalar.dma_start(out=bias_rows[0:1, :], in_=bq.unsqueeze(0))
-        nc.scalar.dma_start(out=bias_rows[1:2, :], in_=bk.unsqueeze(0))
-        nc.scalar.dma_start(out=bias_rows[2:TILES, :], in_=bv.rearrange("(r o) -> r o", o=P))
+        nc.sync.dma_start(out=bias_rows[0:1, :], in_=bq.unsqueeze(0))
+        nc.sync.dma_start(out=bias_rows[1:2, :], in_=bk.unsqueeze(0))
+        nc.sync.dma_start(out=bias_rows[2:TILES, :], in_=bv.rearrange("(r o) -> r o", o=P))
         bias_rows_f32 = const.tile([P, P], F32)
         nc.gpsimd.tensor_copy(out=bias_rows_f32[:], in_=bias_rows[:])
 
@@ -171,25 +173,23 @@ def tile_selfattentionpatch_pa_t_kernel(tc, x, wq, bq, wk, bk, wv, bv, out_0, ou
                 add_bias(m, cols)
                 nc.sync.dma_start(out=out_2[0, (m - 2) * P : (m - 1) * P, cols], in_=result[:, m, cols])
 
+        for m in range(FIRST_WEIGHTS):
+            prepare_weights(m)
         regroup_x(0)
         for g in range(PASSES):
             quantise_x(0, g)
-        for m in range(LEAD):
+        for m in range(FIRST_WEIGHTS, TILES):
             prepare_weights(m)
+        regroup_x(1)
         for j in range(CHUNKS):
             for m in range(TILES):
                 for g in range(PASSES):
                     if m == QUANTISE_AT + 2 * g and j + 1 < CHUNKS:
                         quantise_x(j + 1, g)
                 convolve_and_pool(j, m)
-                if j == 0 and m + LEAD < TILES:
-                    prepare_weights(m + LEAD)
-                if m == LEAD:
-                    if j == 0:
-                        regroup_x(1)
-                    if j + 2 < CHUNKS:
-                        regroup_x(j + 2)
-            if j == 0:
+                if m == 0 and j + 2 < CHUNKS:
+                    regroup_x(j + 2)
+            if j == HALF_CHUNKS - 1:
                 prepare_bias()
             if (j + 1) % HALF_CHUNKS == 0:
                 finish_half(j // HALF_CHUNKS)

@@ -27,6 +27,7 @@ HALVES = 2
 HALF_WINDOWS = WINDOWS // HALVES
 HALF_CHUNKS = CHUNKS // HALVES
 FIRST_WEIGHTS = 4
+EARLY_WEIGHTS = 2
 QUANTISE_AT = 6
 
 FLOPS = 2 * TILES * P * CHANNELS * SIDE * SIDE
@@ -89,7 +90,7 @@ def tile_selfattentionpatch_pa_t_kernel(tc, x, wq, bq, wk, bk, wv, bv, out_0, ou
             flipped = psum_small.tile([P, PASSES * 2 * P], F32, tag="small")
             for s in range(PASSES * 2):
                 nc.tensor.transpose(flipped[:, s * P : (s + 1) * P], words[:, s * P : (s + 1) * P], ident[:])
-            w_grouped = stage.tile([P, PASSES * P * 2], F32, align_bytes=64)
+            w_grouped = loaded.tile([P, PASSES * P * 2], F32, name="w_grouped%d" % m, align_bytes=64)
             nc.scalar.copy(
                 out=w_grouped[:].rearrange("p (g o u) -> p g o u", g=PASSES, u=2),
                 in_=flipped[:].rearrange("p (g u o) -> p g o u", g=PASSES, u=2),
@@ -173,9 +174,11 @@ def tile_selfattentionpatch_pa_t_kernel(tc, x, wq, bq, wk, bk, wv, bv, out_0, ou
                 add_bias(m, cols)
                 nc.sync.dma_start(out=out_2[0, (m - 2) * P : (m - 1) * P, cols], in_=result[:, m, cols])
 
-        for m in range(FIRST_WEIGHTS):
+        for m in range(EARLY_WEIGHTS):
             prepare_weights(m)
         regroup_x(0)
+        for m in range(EARLY_WEIGHTS, FIRST_WEIGHTS):
+            prepare_weights(m)
         for g in range(PASSES):
             quantise_x(0, g)
         for m in range(FIRST_WEIGHTS, TILES):

@@ -28,7 +28,8 @@ HALF_WINDOWS = WINDOWS // HALVES
 HALF_CHUNKS = CHUNKS // HALVES
 FIRST_WEIGHTS = 4
 EARLY_WEIGHTS = 2
-QUANTISE_AT = 6
+ACC_BANKS = 6
+QUANTISE_AT = 4
 
 FLOPS = 2 * TILES * P * CHANNELS * SIDE * SIDE
 
@@ -40,11 +41,12 @@ def tile_selfattentionpatch_pa_t_kernel(tc, x, wq, bq, wk, bk, wv, bv, out_0, ou
         loaded = ctx.enter_context(tc.tile_pool(name="loaded", bufs=1))
         stage = ctx.enter_context(tc.tile_pool(name="stage", bufs=3))
         psum_small = ctx.enter_context(tc.psum_pool(name="psum_small", bufs=2))
-        psum_acc = ctx.enter_context(tc.psum_pool(name="psum_acc", bufs=6))
+        psum_acc = ctx.enter_context(tc.psum_pool(name="psum_acc", bufs=ACC_BANKS))
         ctx.enter_context(tc.manual_schedule())
 
         x_pairs = x[0].rearrange("(s p e) h w -> s p e (h w)", s=PASSES * 2, p=P, e=2)
         w_blocks = [wq, wk] + [wv[i * P : (i + 1) * P, :] for i in range(TILES - 2)]
+        kv_rows = [out_1[0]] + [out_2[0, i * P : (i + 1) * P, :] for i in range(TILES - 2)]
         x_raw = [loaded.tile([P, PASSES * PACK, CHUNK], BF16, name="x_raw%d" % j) for j in range(CHUNKS)]
         w_raw = [loaded.tile([P, CHANNELS], BF16, name="w_raw%d" % m) for m in range(TILES)]
 
@@ -160,19 +162,21 @@ def tile_selfattentionpatch_pa_t_kernel(tc, x, wq, bq, wk, bk, wv, bv, out_0, ou
                 scale=1.0,
             )
 
+        def finish_block(m, cols):
+            add_bias(m, cols)
+            nc.sync.dma_start(out=kv_rows[m - 1][:, cols], in_=result[:, m, cols])
+
         def finish_half(h):
             cols = slice(h * HALF_WINDOWS, (h + 1) * HALF_WINDOWS)
             add_bias(0, cols)
             q_flipped = psum_small.tile([P, P], F32, tag="small")
             nc.tensor.transpose(q_flipped[:], result[:, 0, cols], ident[:])
-            add_bias(1, cols)
-            nc.sync.dma_start(out=out_1[0, :, cols], in_=result[:, 1, cols])
+            for m in range(1, TILES - 1):
+                finish_block(m, cols)
             q_rows = stage.tile([P, P], F32)
             nc.scalar.copy(out=q_rows[:], in_=q_flipped[:])
             nc.sync.dma_start(out=out_0[0, cols, :], in_=q_rows[:])
-            for m in range(2, TILES):
-                add_bias(m, cols)
-                nc.sync.dma_start(out=out_2[0, (m - 2) * P : (m - 1) * P, cols], in_=result[:, m, cols])
+            finish_block(TILES - 1, cols)
 
         for m in range(EARLY_WEIGHTS):
             prepare_weights(m)

@@ -89,7 +89,7 @@ def tile_selfattentionpatch_pa_t_kernel(tc, x, wq, bq, wk, bk, wv, bv, out_0, ou
 
         def prepare_weights(m):
             words = w_raw[m][:].bitcast(F32)
-            flipped = psum_small.tile([P, PASSES * 2 * P], F32, tag="small")
+            flipped = psum_acc.tile([P, PASSES * 2 * P], F32, tag="acc")
             for s in range(PASSES * 2):
                 nc.tensor.transpose(flipped[:, s * P : (s + 1) * P], words[:, s * P : (s + 1) * P], ident[:])
             w_grouped = loaded.tile([P, PASSES * P * 2], F32, name="w_grouped%d" % m, align_bytes=64)

from contextlib import ExitStack

import concourse.mybir as mybir
from concourse.masks import make_identity

F32 = mybir.dt.float32
BF16 = mybir.dt.bfloat16
U32 = mybir.dt.uint32
U8 = mybir.dt.uint8
FP8X4 = mybir.dt.float8_e4m3fn_x4

P = 128
PACK = 4
K_PASS = P * PACK
CHANNELS = 1024
PASSES = CHANNELS // K_PASS
SIDE = 64
POOL = 4
CHUNK = 512
CHUNKS = SIDE * SIDE // CHUNK
CHUNK_BANDS = CHUNK // (SIDE * POOL)
BAND_WINDOWS = SIDE // POOL
CHUNK_WINDOWS = CHUNK_BANDS * BAND_WINDOWS
WINDOWS = CHUNKS * CHUNK_WINDOWS
TILES = 10
HALVES = 2
HALF_WINDOWS = WINDOWS // HALVES
HALF_CHUNKS = CHUNKS // HALVES
FIRST_WEIGHTS = 4
EARLY_WEIGHTS = 2
ACC_BANKS = 6
QUANTISE_AT = 4

FLOPS = 2 * TILES * P * CHANNELS * SIDE * SIDE


def tile_selfattentionpatch_pa_t_kernel(tc, x, wq, bq, wk, bk, wv, bv, out_0, out_1, out_2):
    nc = tc.nc
    with ExitStack() as ctx:
        const = ctx.enter_context(tc.tile_pool(name="const", bufs=1))
        loaded = ctx.enter_context(tc.tile_pool(name="loaded", bufs=1))
        stage = ctx.enter_context(tc.tile_pool(name="stage", bufs=3))
        psum_small = ctx.enter_context(tc.psum_pool(name="psum_small", bufs=2))
        psum_acc = ctx.enter_context(tc.psum_pool(name="psum_acc", bufs=ACC_BANKS))
        ctx.enter_context(tc.manual_schedule())

        x_pairs = x[0].rearrange("(s p e) h w -> s p e (h w)", s=PASSES * 2, p=P, e=2)
        w_blocks = [wq, wk] + [wv[i * P : (i + 1) * P, :] for i in range(TILES - 2)]
        kv_rows = [out_1[0]] + [out_2[0, i * P : (i + 1) * P, :] for i in range(TILES - 2)]
        x_raw = [loaded.tile([P, PASSES * PACK, CHUNK], BF16, name="x_raw%d" % j) for j in range(CHUNKS)]
        w_raw = [loaded.tile([P, CHANNELS], BF16, name="w_raw%d" % m) for m in range(TILES)]

        def load_x(j):
            for s in range(PASSES * 2):
                nc.sync.dma_start(
                    out=x_raw[j][:, 2 * s : 2 * s + 2, :],
                    in_=x_pairs[s][:, :, j * CHUNK : (j + 1) * CHUNK],
                )

        for m in range(FIRST_WEIGHTS):
            nc.sync.dma_start(out=w_raw[m][:], in_=w_blocks[m])
        load_x(0)
        for m in range(FIRST_WEIGHTS, TILES):
            nc.sync.dma_start(out=w_raw[m][:], in_=w_blocks[m])
        for j in range(1, CHUNKS):
            load_x(j)

        ident = const.tile([P, P], F32)
        make_identity(nc, ident[:])

        table_in = const.tile([P, 1], F32)
        table_out = const.tile([P, 1], F32)
        nc.vector.memset(table_in[:], 0.0)
        nc.scalar.activation(out=table_out[:], in_=table_in[:], func=mybir.ActivationFunctionType.Identity)

        bias_rows = const.tile([P, P], BF16)
        nc.gpsimd.memset(bias_rows[:], 0.0)
        nc.sync.dma_start(out=bias_rows[0:1, :], in_=bq.unsqueeze(0))
        nc.sync.dma_start(out=bias_rows[1:2, :], in_=bk.unsqueeze(0))
        nc.sync.dma_start(out=bias_rows[2:TILES, :], in_=bv.rearrange("(r o) -> r o", o=P))
        bias_rows_f32 = const.tile([P, P], F32)
        nc.gpsimd.tensor_copy(out=bias_rows_f32[:], in_=bias_rows[:])

        w_codes = const.tile([P, TILES * PASSES * P], U32, align_bytes=64)
        w_scales = const.tile([P, TILES * PASSES * P], U8, align_bytes=64)
        pooled = const.tile([P, TILES, WINDOWS], F32)
        result = const.tile([P, TILES, WINDOWS], F32)
        bias = const.tile([P, TILES], F32)

        def prepare_weights(m):
            words = w_raw[m][:].bitcast(F32)
            flipped = psum_acc.tile([P, PASSES * 2 * P], F32, tag="acc")
            for s in range(PASSES * 2):
                nc.tensor.transpose(flipped[:, s * P : (s + 1) * P], words[:, s * P : (s + 1) * P], ident[:])
            w_grouped = loaded.tile([P, PASSES * P * 2], F32, name="w_grouped%d" % m, align_bytes=64)
            nc.scalar.copy(
                out=w_grouped[:].rearrange("p (g o u) -> p g o u", g=PASSES, u=2),
                in_=flipped[:].rearrange("p (g u o) -> p g o u", g=PASSES, u=2),
            )
            cols = slice(m * PASSES * P, (m + 1) * PASSES * P)
            nc.vector.quantize_mx(
                out=w_codes[:, cols].bitcast(FP8X4), scales=w_scales[:, cols], in_=w_grouped[:].bitcast(BF16)
            )

        x_grouped = {}
        x_codes = {}
        x_scales = {}

        def regroup_x(j):
            x_grouped[j] = stage.tile([P, PASSES, CHUNK * PACK], BF16, name="x_grouped", align_bytes=64)
            for g in range(PASSES):
                source = x_raw[j][:, g * PACK : (g + 1) * PACK, :].rearrange("p t (c i) -> p c t i", i=4)
                target = x_grouped[j][:, g, :].rearrange("p (c i t) -> p c t i", i=4, t=PACK)
                if j == 0:
                    nc.vector.tensor_copy(out=target, in_=source)
                else:
                    nc.scalar.copy(out=target, in_=source)

        def quantise_x(j, g):
            if g == 0:
                x_codes[j] = stage.tile([P, PASSES * CHUNK], U32, name="x_codes", align_bytes=64)
                x_scales[j] = stage.tile([P, PASSES * CHUNK], U8, name="x_scales", align_bytes=64)
            x_cols = slice(g * CHUNK, (g + 1) * CHUNK)
            nc.vector.quantize_mx(
                out=x_codes[j][:, x_cols].bitcast(FP8X4), scales=x_scales[j][:, x_cols], in_=x_grouped[j][:, g, :]
            )

        def convolve_and_pool(j, m):
            acc = psum_acc.tile([P, CHUNK], F32)
            for g in range(PASSES):
                w_cols = slice((m * PASSES + g) * P, (m * PASSES + g + 1) * P)
                x_cols = slice(g * CHUNK, (g + 1) * CHUNK)
                nc.tensor.matmul_mx(
                    out=acc[:],
                    lhsT=w_codes[:, w_cols].bitcast(FP8X4),
                    lhsT_scale=w_scales[:, w_cols],
                    rhs=x_codes[j][:, x_cols].bitcast(FP8X4),
                    rhs_scale=x_scales[j][:, x_cols],
                    start=(g == 0),
                    stop=(g == PASSES - 1),
                )
            nc.vector.tensor_reduce(
                out=pooled[:, m, j * CHUNK_WINDOWS : (j + 1) * CHUNK_WINDOWS].rearrange(
                    "p (a b) -> p a b", a=CHUNK_BANDS
                ),
                in_=acc[:].rearrange("p (a di b dj) -> p a b di dj", a=CHUNK_BANDS, di=POOL, dj=POOL),
                axis=mybir.AxisListType.XY,
                op=mybir.AluOpType.max,
            )

        def prepare_bias():
            bias_flipped = psum_small.tile([P, P], F32, tag="small")
            nc.tensor.transpose(bias_flipped[:], bias_rows_f32[:], ident[:])
            nc.scalar.copy(out=bias[:], in_=bias_flipped[:, 0:TILES])

        def add_bias(m, cols):
            nc.scalar.activation(
                out=result[:, m, cols],
                in_=pooled[:, m, cols],
                func=mybir.ActivationFunctionType.Identity,
                bias=bias[:, m : m + 1],
                scale=1.0,
            )

        def finish_block(m, cols):
            add_bias(m, cols)
            nc.sync.dma_start(out=kv_rows[m - 1][:, cols], in_=result[:, m, cols])

        def finish_half(h):
            cols = slice(h * HALF_WINDOWS, (h + 1) * HALF_WINDOWS)
            add_bias(0, cols)
            q_flipped = psum_small.tile([P, P], F32, tag="small")
            nc.tensor.transpose(q_flipped[:], result[:, 0, cols], ident[:])
            for m in range(1, TILES - 1):
                finish_block(m, cols)
            q_rows = stage.tile([P, P], F32)
            nc.scalar.copy(out=q_rows[:], in_=q_flipped[:])
            nc.sync.dma_start(out=out_0[0, cols, :], in_=q_rows[:])
            finish_block(TILES - 1, cols)

        for m in range(EARLY_WEIGHTS):
            prepare_weights(m)
        regroup_x(0)
        for m in range(EARLY_WEIGHTS, FIRST_WEIGHTS):
            prepare_weights(m)
        for g in range(PASSES):
            quantise_x(0, g)
        for m in range(FIRST_WEIGHTS, TILES):
            prepare_weights(m)
        regroup_x(1)
        for j in range(CHUNKS):
            for m in range(TILES):
                for g in range(PASSES):
                    if m == QUANTISE_AT + 2 * g and j + 1 < CHUNKS:
                        quantise_x(j + 1, g)
                convolve_and_pool(j, m)
                if m == 0 and j + 2 < CHUNKS:
                    regroup_x(j + 2)
            if j == HALF_CHUNKS - 1:
                prepare_bias()
            if (j + 1) % HALF_CHUNKS == 0:
                finish_half(j // HALF_CHUNKS)
